import numpy as np
import ml_dtypes

BF16 = ml_dtypes.bfloat16


def bf(x):
    return np.asarray(x, np.float32).astype(BF16)


def f32(x):
    return np.asarray(x, np.float32)


def f64(x):
    return np.asarray(x).astype(np.float64)


def striped(idx):
    return np.tile(idx.reshape(-1, 16).T, (8, 1))


B, E, Q, F, D, M, S, K, N, H, R = 32, 96, 97, 4, 128, 128, 4096, 2, 8192, 2048, 4
SLOPE = 0.2


def leaky(v):
    return np.maximum(v, SLOPE * v)


def setup_inputs():
    table = bf(np.random.standard_normal((D, S)))
    wx = np.random.standard_normal((1, F)) / np.sqrt(Q)
    we = np.random.standard_normal((E, F)) / np.sqrt(Q)
    w = bf(np.concatenate([np.kron(np.eye(B), wx), np.tile(we, (1, B))], axis=0))
    b = f32(np.tile(0.3 * np.random.standard_normal((F, 1)), (B, 1)))
    idx = np.concatenate([np.random.permutation(S)[:H] for _ in range(R)])
    return {"table": table, "w": w, "b": b, "offs": striped(idx)}


def reference(table, w, b, offs):
    idx = offs[:16].T.reshape(-1)
    t = f64(table)
    ww = f64(w)
    centre = leaky(ww.T @ t + f64(b))
    nb = leaky(ww.T @ t[:, idx] + f64(b))
    d = np.tile(centre, (1, K)) - nb
    return d * d

@@ -1,0 +1,69 @@
+import concourse.mybir as mybir
+
+P = 128
+NODES = 4096
+ENTRIES = 8192
+PIECE = 512
+PIECE_OFFSET_COLUMNS = PIECE // 16
+CENTRE_PIECES = NODES // PIECE
+LIST_PIECES = ENTRIES // PIECE
+LOAD_COLUMNS = 1024
+
+FLOPS = 2 * P * P * (NODES + ENTRIES)
+
+BF16, F32, U16 = mybir.dt.bfloat16, mybir.dt.float32, mybir.dt.uint16
+ALU = mybir.AluOpType
+FUNC = mybir.ActivationFunctionType
+
+
+def tile_graphlearningmodule_kernel(tc, table, w, b, offs, out):
+    nc = tc.nc
+    with (
+        tc.tile_pool(name="held", bufs=1) as held,
+        tc.tile_pool(name="work", bufs=3) as work,
+        tc.psum_pool(name="banks", bufs=8) as banks,
+    ):
+        weights = held.tile([P, P], BF16, name="weights")
+        nc.scalar.dma_start(weights[:], w)
+        bias = held.tile([P, 1], F32, name="bias")
+        nc.scalar.dma_start(bias[:], b)
+        window = held.tile([P, NODES], BF16, name="window")
+        for first in range(0, NODES, LOAD_COLUMNS):
+            columns = slice(first, first + LOAD_COLUMNS)
+            nc.sync.dma_start(window[:, columns], table[:, columns])
+        offsets = held.tile([P, ENTRIES // 16], U16, name="offsets")
+        nc.sync.dma_start(offsets[:], offs)
+
+        minus_bias = held.tile([P, 1], F32, name="minus_bias")
+        nc.vector.tensor_scalar_mul(minus_bias[:], bias[:], -1.0)
+
+        h_centre = held.tile([P, NODES], F32, name="h_centre")
+        for c in range(CENTRE_PIECES):
+            columns = slice(c * PIECE, (c + 1) * PIECE)
+            product = banks.tile([P, PIECE], F32, name="product")
+            nc.tensor.matmul(product[:], weights[:], window[:, columns], start=True, stop=True)
+            quarter = work.tile([P, PIECE], F32, name="quarter")
+            nc.scalar.activation(quarter[:], product[:], FUNC.Copy, scale=0.25)
+            nc.vector.scalar_tensor_tensor(
+                h_centre[:, columns], product[:], minus_bias[:], quarter[:], op0=ALU.max, op1=ALU.add
+            )
+
+        for k in range(LIST_PIECES):
+            c = k % CENTRE_PIECES
+            looked_up = window[:].indirect(
+                offsets[:, k * PIECE_OFFSET_COLUMNS : (k + 1) * PIECE_OFFSET_COLUMNS]
+            )
+            product = banks.tile([P, PIECE], F32, name="product")
+            nc.tensor.matmul(product[:], weights[:], looked_up, start=True, stop=True)
+            linear = work.tile([P, PIECE], F32, name="linear")
+            nc.vector.scalar_tensor_tensor(
+                linear[:], product[:], 0.25, h_centre[:, c * PIECE : (c + 1) * PIECE],
+                op0=ALU.mult, op1=ALU.subtract,
+            )
+            difference = work.tile([P, PIECE], F32, name="difference")
+            nc.vector.scalar_tensor_tensor(
+                difference[:], product[:], minus_bias[:], linear[:], op0=ALU.max, op1=ALU.add
+            )
+            squared = work.tile([P, PIECE], F32, name="squared")
+            nc.scalar.activation(squared[:], difference[:], FUNC.Square, scale=0.8)
+            nc.sync.dma_start(out[:, k * PIECE : (k + 1) * PIECE], squared[:])

@@ -20,7 +20,7 @@ def tile_graphlearningmodule_kernel(tc, table, w, b, offs, out):
     nc = tc.nc
     with (
         tc.tile_pool(name="held", bufs=1) as held,
-        tc.tile_pool(name="work", bufs=3) as work,
+        tc.tile_pool(name="work", bufs=4) as work,
         tc.psum_pool(name="banks", bufs=8) as banks,
     ):
         weights = held.tile([P, P], BF16, name="weights")
@@ -55,15 +55,26 @@ def tile_graphlearningmodule_kernel(tc, table, w, b, offs, out):
             )
             product = banks.tile([P, PIECE], F32, name="product")
             nc.tensor.matmul(product[:], weights[:], looked_up, start=True, stop=True)
-            linear = work.tile([P, PIECE], F32, name="linear")
-            nc.vector.scalar_tensor_tensor(
-                linear[:], product[:], 0.25, h_centre[:, c * PIECE : (c + 1) * PIECE],
-                op0=ALU.mult, op1=ALU.subtract,
-            )
             difference = work.tile([P, PIECE], F32, name="difference")
-            nc.vector.scalar_tensor_tensor(
-                difference[:], product[:], minus_bias[:], linear[:], op0=ALU.max, op1=ALU.add
-            )
+            if k % 2 == 1:
+                linear = work.tile([P, PIECE], F32, name="linear")
+                nc.vector.scalar_tensor_tensor(
+                    linear[:], product[:], 0.25, h_centre[:, c * PIECE : (c + 1) * PIECE],
+                    op0=ALU.mult, op1=ALU.subtract,
+                )
+                nc.vector.scalar_tensor_tensor(
+                    difference[:], product[:], minus_bias[:], linear[:], op0=ALU.max, op1=ALU.add
+                )
+            else:
+                quarter = work.tile([P, PIECE], F32, name="quarter")
+                nc.scalar.activation(quarter[:], product[:], FUNC.Copy, scale=0.25)
+                h_piece = work.tile([P, PIECE], F32, name="h_piece")
+                nc.vector.scalar_tensor_tensor(
+                    h_piece[:], product[:], minus_bias[:], quarter[:], op0=ALU.max, op1=ALU.add
+                )
+                nc.gpsimd.tensor_tensor(
+                    difference[:], h_piece[:], h_centre[:, c * PIECE : (c + 1) * PIECE], ALU.subtract
+                )
             squared = work.tile([P, PIECE], F32, name="squared")
             nc.scalar.activation(squared[:], difference[:], FUNC.Square, scale=0.8)
             nc.sync.dma_start(out[:, k * PIECE : (k + 1) * PIECE], squared[:])

@@ -34,6 +34,10 @@ def tile_graphlearningmodule_kernel(tc, table, w, b, offs, out):
         offsets = held.tile([P, ENTRIES // 16], U16, name="offsets")
         nc.sync.dma_start(offsets[:], offs)
 
+        scratch = held.tile([P, 1], F32, name="scratch")
+        nc.vector.memset(scratch[:], 0.0)
+        nc.scalar.activation(scratch[:], scratch[:], FUNC.Square)
+
         minus_bias = held.tile([P, 1], F32, name="minus_bias")
         nc.vector.tensor_scalar_mul(minus_bias[:], bias[:], -1.0)
 

@@ -35,11 +35,11 @@ def tile_graphlearningmodule_kernel(tc, table, w, b, offs, out):
         nc.sync.dma_start(offsets[:], offs)
 
         scratch = held.tile([P, 1], F32, name="scratch")
-        nc.vector.memset(scratch[:], 0.0)
+        nc.gpsimd.memset(scratch[:], 0.0)
         nc.scalar.activation(scratch[:], scratch[:], FUNC.Square)
 
         minus_bias = held.tile([P, 1], F32, name="minus_bias")
-        nc.vector.tensor_scalar_mul(minus_bias[:], bias[:], -1.0)
+        nc.gpsimd.tensor_scalar_mul(minus_bias[:], bias[:], -1.0)
 
         h_centre = held.tile([P, NODES], F32, name="h_centre")
         for c in range(CENTRE_PIECES):
@@ -79,6 +79,6 @@ def tile_graphlearningmodule_kernel(tc, table, w, b, offs, out):
                 nc.gpsimd.tensor_tensor(
                     difference[:], h_piece[:], h_centre[:, c * PIECE : (c + 1) * PIECE], ALU.subtract
                 )
-            squared = work.tile([P, PIECE], F32, name="squared")
+            squared = work.tile([P, PIECE], F32, name="squared", bufs=16)
             nc.scalar.activation(squared[:], difference[:], FUNC.Square, scale=0.8)
             nc.sync.dma_start(out[:, k * PIECE : (k + 1) * PIECE], squared[:])

@@ -7,6 +7,7 @@ PIECE = 512
 PIECE_OFFSET_COLUMNS = PIECE // 16
 CENTRE_PIECES = NODES // PIECE
 LIST_PIECES = ENTRIES // PIECE
+PAIRS = LIST_PIECES // 2
 LOAD_COLUMNS = 1024
 
 FLOPS = 2 * P * P * (NODES + ENTRIES)
@@ -52,33 +53,35 @@ def tile_graphlearningmodule_kernel(tc, table, w, b, offs, out):
                 h_centre[:, columns], product[:], minus_bias[:], quarter[:], op0=ALU.max, op1=ALU.add
             )
 
-        for k in range(LIST_PIECES):
-            c = k % CENTRE_PIECES
-            looked_up = window[:].indirect(
-                offsets[:, k * PIECE_OFFSET_COLUMNS : (k + 1) * PIECE_OFFSET_COLUMNS]
+        for pair in range(PAIRS):
+            products, centres, differences = [], [], []
+            for k in (2 * pair, 2 * pair + 1):
+                looked_up = window[:].indirect(
+                    offsets[:, k * PIECE_OFFSET_COLUMNS : (k + 1) * PIECE_OFFSET_COLUMNS]
+                )
+                product = banks.tile([P, PIECE], F32, name="product")
+                nc.tensor.matmul(product[:], weights[:], looked_up, start=True, stop=True)
+                products.append(product)
+                c = k % CENTRE_PIECES
+                centres.append(h_centre[:, c * PIECE : (c + 1) * PIECE])
+                differences.append(work.tile([P, PIECE], F32, name="difference"))
+
+            quarter = work.tile([P, PIECE], F32, name="quarter")
+            nc.scalar.activation(quarter[:], products[0][:], FUNC.Copy, scale=0.25)
+            linear = work.tile([P, PIECE], F32, name="linear")
+            nc.vector.scalar_tensor_tensor(
+                linear[:], products[1][:], 0.25, centres[1], op0=ALU.mult, op1=ALU.subtract
             )
-            product = banks.tile([P, PIECE], F32, name="product")
-            nc.tensor.matmul(product[:], weights[:], looked_up, start=True, stop=True)
-            difference = work.tile([P, PIECE], F32, name="difference")
-            if k % 2 == 1:
-                linear = work.tile([P, PIECE], F32, name="linear")
-                nc.vector.scalar_tensor_tensor(
-                    linear[:], product[:], 0.25, h_centre[:, c * PIECE : (c + 1) * PIECE],
-                    op0=ALU.mult, op1=ALU.subtract,
-                )
-                nc.vector.scalar_tensor_tensor(
-                    difference[:], product[:], minus_bias[:], linear[:], op0=ALU.max, op1=ALU.add
-                )
-            else:
-                quarter = work.tile([P, PIECE], F32, name="quarter")
-                nc.scalar.activation(quarter[:], product[:], FUNC.Copy, scale=0.25)
-                h_piece = work.tile([P, PIECE], F32, name="h_piece")
-                nc.vector.scalar_tensor_tensor(
-                    h_piece[:], product[:], minus_bias[:], quarter[:], op0=ALU.max, op1=ALU.add
-                )
-                nc.gpsimd.tensor_tensor(
-                    difference[:], h_piece[:], h_centre[:, c * PIECE : (c + 1) * PIECE], ALU.subtract
-                )
-            squared = work.tile([P, PIECE], F32, name="squared", bufs=16)
-            nc.scalar.activation(squared[:], difference[:], FUNC.Square, scale=0.8)
-            nc.sync.dma_start(out[:, k * PIECE : (k + 1) * PIECE], squared[:])
+            h_piece = work.tile([P, PIECE], F32, name="h_piece")
+            nc.vector.scalar_tensor_tensor(
+                h_piece[:], products[0][:], minus_bias[:], quarter[:], op0=ALU.max, op1=ALU.add
+            )
+            nc.gpsimd.tensor_tensor(differences[0][:], h_piece[:], centres[0], ALU.subtract)
+            nc.vector.scalar_tensor_tensor(
+                differences[1][:], products[1][:], minus_bias[:], linear[:], op0=ALU.max, op1=ALU.add
+            )
+
+            for k, difference in ((2 * pair + 1, differences[1]), (2 * pair, differences[0])):
+                squared = work.tile([P, PIECE], F32, name="squared", bufs=16)
+                nc.scalar.activation(squared[:], difference[:], FUNC.Square, scale=0.8)
+                nc.sync.dma_start(out[:, k * PIECE : (k + 1) * PIECE], squared[:])

@@ -7,8 +7,7 @@ PIECE = 512
 PIECE_OFFSET_COLUMNS = PIECE // 16
 CENTRE_PIECES = NODES // PIECE
 LIST_PIECES = ENTRIES // PIECE
-PAIRS = LIST_PIECES // 2
-LOAD_COLUMNS = 1024
+LOAD_COLUMNS = 512
 
 FLOPS = 2 * P * P * (NODES + ENTRIES)
 
@@ -21,7 +20,7 @@ def tile_graphlearningmodule_kernel(tc, table, w, b, offs, out):
     nc = tc.nc
     with (
         tc.tile_pool(name="held", bufs=1) as held,
-        tc.tile_pool(name="work", bufs=4) as work,
+        tc.tile_pool(name="work", bufs=16) as work,
         tc.psum_pool(name="banks", bufs=8) as banks,
     ):
         weights = held.tile([P, P], BF16, name="weights")
@@ -53,35 +52,33 @@ def tile_graphlearningmodule_kernel(tc, table, w, b, offs, out):
                 h_centre[:, columns], product[:], minus_bias[:], quarter[:], op0=ALU.max, op1=ALU.add
             )
 
-        for pair in range(PAIRS):
-            products, centres, differences = [], [], []
-            for k in (2 * pair, 2 * pair + 1):
-                looked_up = window[:].indirect(
-                    offsets[:, k * PIECE_OFFSET_COLUMNS : (k + 1) * PIECE_OFFSET_COLUMNS]
+        for k in range(LIST_PIECES):
+            c = k % CENTRE_PIECES
+            looked_up = window[:].indirect(
+                offsets[:, k * PIECE_OFFSET_COLUMNS : (k + 1) * PIECE_OFFSET_COLUMNS]
+            )
+            product = banks.tile([P, PIECE], F32, name="product")
+            nc.tensor.matmul(product[:], weights[:], looked_up, start=True, stop=True)
+            difference = work.tile([P, PIECE], F32, name="difference")
+            if k % 2 == 1:
+                linear = work.tile([P, PIECE], F32, name="linear")
+                nc.vector.scalar_tensor_tensor(
+                    linear[:], product[:], 0.25, h_centre[:, c * PIECE : (c + 1) * PIECE],
+                    op0=ALU.mult, op1=ALU.subtract,
                 )
-                product = banks.tile([P, PIECE], F32, name="product")
-                nc.tensor.matmul(product[:], weights[:], looked_up, start=True, stop=True)
-                products.append(product)
-                c = k % CENTRE_PIECES
-                centres.append(h_centre[:, c * PIECE : (c + 1) * PIECE])
-                differences.append(work.tile([P, PIECE], F32, name="difference"))
-
-            quarter = work.tile([P, PIECE], F32, name="quarter")
-            nc.scalar.activation(quarter[:], products[0][:], FUNC.Copy, scale=0.25)
-            linear = work.tile([P, PIECE], F32, name="linear")
-            nc.vector.scalar_tensor_tensor(
-                linear[:], products[1][:], 0.25, centres[1], op0=ALU.mult, op1=ALU.subtract
-            )
-            h_piece = work.tile([P, PIECE], F32, name="h_piece")
-            nc.vector.scalar_tensor_tensor(
-                h_piece[:], products[0][:], minus_bias[:], quarter[:], op0=ALU.max, op1=ALU.add
-            )
-            nc.gpsimd.tensor_tensor(differences[0][:], h_piece[:], centres[0], ALU.subtract)
-            nc.vector.scalar_tensor_tensor(
-                differences[1][:], products[1][:], minus_bias[:], linear[:], op0=ALU.max, op1=ALU.add
-            )
-
-            for k, difference in ((2 * pair + 1, differences[1]), (2 * pair, differences[0])):
-                squared = work.tile([P, PIECE], F32, name="squared", bufs=16)
-                nc.scalar.activation(squared[:], difference[:], FUNC.Square, scale=0.8)
-                nc.sync.dma_start(out[:, k * PIECE : (k + 1) * PIECE], squared[:])
+                nc.vector.scalar_tensor_tensor(
+                    difference[:], product[:], minus_bias[:], linear[:], op0=ALU.max, op1=ALU.add
+                )
+            else:
+                quarter = work.tile([P, PIECE], F32, name="quarter")
+                nc.scalar.activation(quarter[:], product[:], FUNC.Copy, scale=0.25)
+                h_piece = work.tile([P, PIECE], F32, name="h_piece")
+                nc.vector.scalar_tensor_tensor(
+                    h_piece[:], product[:], minus_bias[:], quarter[:], op0=ALU.max, op1=ALU.add
+                )
+                nc.gpsimd.tensor_tensor(
+                    difference[:], h_piece[:], h_centre[:, c * PIECE : (c + 1) * PIECE], ALU.subtract
+                )
+            squared = work.tile([P, PIECE], F32, name="squared")
+            nc.scalar.activation(squared[:], difference[:], FUNC.Square, scale=0.8)
+            nc.sync.dma_start(out[:, k * PIECE : (k + 1) * PIECE], squared[:])

@@ -7,7 +7,6 @@ PIECE = 512
 PIECE_OFFSET_COLUMNS = PIECE // 16
 CENTRE_PIECES = NODES // PIECE
 LIST_PIECES = ENTRIES // PIECE
-LOAD_COLUMNS = 512
 
 FLOPS = 2 * P * P * (NODES + ENTRIES)
 
@@ -20,7 +19,7 @@ def tile_graphlearningmodule_kernel(tc, table, w, b, offs, out):
     nc = tc.nc
     with (
         tc.tile_pool(name="held", bufs=1) as held,
-        tc.tile_pool(name="work", bufs=16) as work,
+        tc.tile_pool(name="work", bufs=LIST_PIECES) as work,
         tc.psum_pool(name="banks", bufs=8) as banks,
     ):
         weights = held.tile([P, P], BF16, name="weights")
@@ -28,8 +27,8 @@ def tile_graphlearningmodule_kernel(tc, table, w, b, offs, out):
         bias = held.tile([P, 1], F32, name="bias")
         nc.scalar.dma_start(bias[:], b)
         window = held.tile([P, NODES], BF16, name="window")
-        for first in range(0, NODES, LOAD_COLUMNS):
-            columns = slice(first, first + LOAD_COLUMNS)
+        for c in range(CENTRE_PIECES):
+            columns = slice(c * PIECE, (c + 1) * PIECE)
             nc.sync.dma_start(window[:, columns], table[:, columns])
         offsets = held.tile([P, ENTRIES // 16], U16, name="offsets")
         nc.sync.dma_start(offsets[:], offs)
@@ -40,16 +39,18 @@ def tile_graphlearningmodule_kernel(tc, table, w, b, offs, out):
 
         minus_bias = held.tile([P, 1], F32, name="minus_bias")
         nc.gpsimd.tensor_scalar_mul(minus_bias[:], bias[:], -1.0)
+        bias_scaled = held.tile([P, 1], F32, name="bias_scaled")
+        nc.gpsimd.tensor_scalar_mul(bias_scaled[:], bias[:], 0.8)
 
         h_centre = held.tile([P, NODES], F32, name="h_centre")
         for c in range(CENTRE_PIECES):
             columns = slice(c * PIECE, (c + 1) * PIECE)
             product = banks.tile([P, PIECE], F32, name="product")
             nc.tensor.matmul(product[:], weights[:], window[:, columns], start=True, stop=True)
-            quarter = work.tile([P, PIECE], F32, name="quarter")
-            nc.scalar.activation(quarter[:], product[:], FUNC.Copy, scale=0.25)
+            positive = work.tile([P, PIECE], F32, name="positive")
+            nc.scalar.activation(positive[:], product[:], FUNC.Relu, bias=bias[:])
             nc.vector.scalar_tensor_tensor(
-                h_centre[:, columns], product[:], minus_bias[:], quarter[:], op0=ALU.max, op1=ALU.add
+                h_centre[:, columns], product[:], 0.25, positive[:], op0=ALU.mult, op1=ALU.add
             )
 
         for k in range(LIST_PIECES):
@@ -60,6 +61,7 @@ def tile_graphlearningmodule_kernel(tc, table, w, b, offs, out):
             product = banks.tile([P, PIECE], F32, name="product")
             nc.tensor.matmul(product[:], weights[:], looked_up, start=True, stop=True)
             difference = work.tile([P, PIECE], F32, name="difference")
+            squared = work.tile([P, PIECE], F32, name="squared")
             if k % 2 == 1:
                 linear = work.tile([P, PIECE], F32, name="linear")
                 nc.vector.scalar_tensor_tensor(
@@ -69,16 +71,18 @@ def tile_graphlearningmodule_kernel(tc, table, w, b, offs, out):
                 nc.vector.scalar_tensor_tensor(
                     difference[:], product[:], minus_bias[:], linear[:], op0=ALU.max, op1=ALU.add
                 )
+                nc.scalar.activation(
+                    squared[:], difference[:], FUNC.Square, bias=bias_scaled[:], scale=0.8
+                )
             else:
-                quarter = work.tile([P, PIECE], F32, name="quarter")
-                nc.scalar.activation(quarter[:], product[:], FUNC.Copy, scale=0.25)
+                positive = work.tile([P, PIECE], F32, name="positive")
+                nc.scalar.activation(positive[:], product[:], FUNC.Relu, bias=bias[:])
                 h_piece = work.tile([P, PIECE], F32, name="h_piece")
                 nc.vector.scalar_tensor_tensor(
-                    h_piece[:], product[:], minus_bias[:], quarter[:], op0=ALU.max, op1=ALU.add
+                    h_piece[:], product[:], 0.25, positive[:], op0=ALU.mult, op1=ALU.add
                 )
                 nc.gpsimd.tensor_tensor(
                     difference[:], h_piece[:], h_centre[:, c * PIECE : (c + 1) * PIECE], ALU.subtract
                 )
-            squared = work.tile([P, PIECE], F32, name="squared")
-            nc.scalar.activation(squared[:], difference[:], FUNC.Square, scale=0.8)
+                nc.scalar.activation(squared[:], difference[:], FUNC.Square, scale=0.8)
             nc.sync.dma_start(out[:, k * PIECE : (k + 1) * PIECE], squared[:])

@@ -7,6 +7,7 @@ PIECE = 512
 PIECE_OFFSET_COLUMNS = PIECE // 16
 CENTRE_PIECES = NODES // PIECE
 LIST_PIECES = ENTRIES // PIECE
+LAST_PIECE_SLICES = 4
 
 FLOPS = 2 * P * P * (NODES + ENTRIES)
 
@@ -60,20 +61,28 @@ def tile_graphlearningmodule_kernel(tc, table, w, b, offs, out):
             )
             product = banks.tile([P, PIECE], F32, name="product")
             nc.tensor.matmul(product[:], weights[:], looked_up, start=True, stop=True)
-            difference = work.tile([P, PIECE], F32, name="difference")
-            squared = work.tile([P, PIECE], F32, name="squared")
-            if k % 2 == 1:
+            if k % 2 == 1 or k == LIST_PIECES - 2:
                 linear = work.tile([P, PIECE], F32, name="linear")
                 nc.vector.scalar_tensor_tensor(
                     linear[:], product[:], 0.25, h_centre[:, c * PIECE : (c + 1) * PIECE],
                     op0=ALU.mult, op1=ALU.subtract,
                 )
-                nc.vector.scalar_tensor_tensor(
-                    difference[:], product[:], minus_bias[:], linear[:], op0=ALU.max, op1=ALU.add
-                )
-                nc.scalar.activation(
-                    squared[:], difference[:], FUNC.Square, bias=bias_scaled[:], scale=0.8
-                )
+                slices = LAST_PIECE_SLICES if k == LIST_PIECES - 1 else 1
+                width = PIECE // slices
+                for s in range(slices):
+                    inside = slice(s * width, (s + 1) * width)
+                    difference = work.tile([P, width], F32, name="difference")
+                    nc.vector.scalar_tensor_tensor(
+                        difference[:], product[:, inside], minus_bias[:], linear[:, inside],
+                        op0=ALU.max, op1=ALU.add,
+                    )
+                    squared = work.tile([P, width], F32, name="squared")
+                    nc.scalar.activation(
+                        squared[:], difference[:], FUNC.Square, bias=bias_scaled[:], scale=0.8
+                    )
+                    nc.sync.dma_start(
+                        out[:, k * PIECE + s * width : k * PIECE + (s + 1) * width], squared[:]
+                    )
             else:
                 positive = work.tile([P, PIECE], F32, name="positive")
                 nc.scalar.activation(positive[:], product[:], FUNC.Relu, bias=bias[:])
@@ -81,8 +90,10 @@ def tile_graphlearningmodule_kernel(tc, table, w, b, offs, out):
                 nc.vector.scalar_tensor_tensor(
                     h_piece[:], product[:], 0.25, positive[:], op0=ALU.mult, op1=ALU.add
                 )
+                difference = work.tile([P, PIECE], F32, name="difference")
                 nc.gpsimd.tensor_tensor(
                     difference[:], h_piece[:], h_centre[:, c * PIECE : (c + 1) * PIECE], ALU.subtract
                 )
+                squared = work.tile([P, PIECE], F32, name="squared")
                 nc.scalar.activation(squared[:], difference[:], FUNC.Square, scale=0.8)
-            nc.sync.dma_start(out[:, k * PIECE : (k + 1) * PIECE], squared[:])
+                nc.sync.dma_start(out[:, k * PIECE : (k + 1) * PIECE], squared[:])

@@ -7,6 +7,8 @@ PIECE = 512
 PIECE_OFFSET_COLUMNS = PIECE // 16
 CENTRE_PIECES = NODES // PIECE
 LIST_PIECES = ENTRIES // PIECE
+GPSIMD_ROAD_PIECES = LIST_PIECES // 2
+TAIL_PIECES = 2
 LAST_PIECE_SLICES = 4
 
 FLOPS = 2 * P * P * (NODES + ENTRIES)
@@ -54,6 +56,7 @@ def tile_graphlearningmodule_kernel(tc, table, w, b, offs, out):
                 h_centre[:, columns], product[:], 0.25, positive[:], op0=ALU.mult, op1=ALU.add
             )
 
+        spread_over = LIST_PIECES - TAIL_PIECES
         for k in range(LIST_PIECES):
             c = k % CENTRE_PIECES
             looked_up = window[:].indirect(
@@ -61,7 +64,7 @@ def tile_graphlearningmodule_kernel(tc, table, w, b, offs, out):
             )
             product = banks.tile([P, PIECE], F32, name="product")
             nc.tensor.matmul(product[:], weights[:], looked_up, start=True, stop=True)
-            if k % 2 == 1 or k == LIST_PIECES - 2:
+            if k >= spread_over or (k * GPSIMD_ROAD_PIECES) % spread_over >= GPSIMD_ROAD_PIECES:
                 linear = work.tile([P, PIECE], F32, name="linear")
                 nc.vector.scalar_tensor_tensor(
                     linear[:], product[:], 0.25, h_centre[:, c * PIECE : (c + 1) * PIECE],

import concourse.mybir as mybir

P = 128
NODES = 4096
ENTRIES = 8192
PIECE = 512
PIECE_OFFSET_COLUMNS = PIECE // 16
CENTRE_PIECES = NODES // PIECE
LIST_PIECES = ENTRIES // PIECE
GPSIMD_ROAD_PIECES = LIST_PIECES // 2
TAIL_PIECES = 2
LAST_PIECE_SLICES = 4

FLOPS = 2 * P * P * (NODES + ENTRIES)

BF16, F32, U16 = mybir.dt.bfloat16, mybir.dt.float32, mybir.dt.uint16
ALU = mybir.AluOpType
FUNC = mybir.ActivationFunctionType


def tile_graphlearningmodule_kernel(tc, table, w, b, offs, out):
    nc = tc.nc
    with (
        tc.tile_pool(name="held", bufs=1) as held,
        tc.tile_pool(name="work", bufs=LIST_PIECES) as work,
        tc.psum_pool(name="banks", bufs=8) as banks,
    ):
        weights = held.tile([P, P], BF16, name="weights")
        nc.scalar.dma_start(weights[:], w)
        bias = held.tile([P, 1], F32, name="bias")
        nc.scalar.dma_start(bias[:], b)
        window = held.tile([P, NODES], BF16, name="window")
        for c in range(CENTRE_PIECES):
            columns = slice(c * PIECE, (c + 1) * PIECE)
            nc.sync.dma_start(window[:, columns], table[:, columns])
        offsets = held.tile([P, ENTRIES // 16], U16, name="offsets")
        nc.sync.dma_start(offsets[:], offs)

        scratch = held.tile([P, 1], F32, name="scratch")
        nc.gpsimd.memset(scratch[:], 0.0)
        nc.scalar.activation(scratch[:], scratch[:], FUNC.Square)

        minus_bias = held.tile([P, 1], F32, name="minus_bias")
        nc.gpsimd.tensor_scalar_mul(minus_bias[:], bias[:], -1.0)
        bias_scaled = held.tile([P, 1], F32, name="bias_scaled")
        nc.gpsimd.tensor_scalar_mul(bias_scaled[:], bias[:], 0.8)

        h_centre = held.tile([P, NODES], F32, name="h_centre")
        for c in range(CENTRE_PIECES):
            columns = slice(c * PIECE, (c + 1) * PIECE)
            product = banks.tile([P, PIECE], F32, name="product")
            nc.tensor.matmul(product[:], weights[:], window[:, columns], start=True, stop=True)
            positive = work.tile([P, PIECE], F32, name="positive")
            nc.scalar.activation(positive[:], product[:], FUNC.Relu, bias=bias[:])
            nc.vector.scalar_tensor_tensor(
                h_centre[:, columns], product[:], 0.25, positive[:], op0=ALU.mult, op1=ALU.add
            )

        spread_over = LIST_PIECES - TAIL_PIECES
        for k in range(LIST_PIECES):
            c = k % CENTRE_PIECES
            looked_up = window[:].indirect(
                offsets[:, k * PIECE_OFFSET_COLUMNS : (k + 1) * PIECE_OFFSET_COLUMNS]
            )
            product = banks.tile([P, PIECE], F32, name="product")
            nc.tensor.matmul(product[:], weights[:], looked_up, start=True, stop=True)
            if k >= spread_over or (k * GPSIMD_ROAD_PIECES) % spread_over >= GPSIMD_ROAD_PIECES:
                linear = work.tile([P, PIECE], F32, name="linear")
                nc.vector.scalar_tensor_tensor(
                    linear[:], product[:], 0.25, h_centre[:, c * PIECE : (c + 1) * PIECE],
                    op0=ALU.mult, op1=ALU.subtract,
                )
                slices = LAST_PIECE_SLICES if k == LIST_PIECES - 1 else 1
                width = PIECE // slices
                for s in range(slices):
                    inside = slice(s * width, (s + 1) * width)
                    difference = work.tile([P, width], F32, name="difference")
                    nc.vector.scalar_tensor_tensor(
                        difference[:], product[:, inside], minus_bias[:], linear[:, inside],
                        op0=ALU.max, op1=ALU.add,
                    )
                    squared = work.tile([P, width], F32, name="squared")
                    nc.scalar.activation(
                        squared[:], difference[:], FUNC.Square, bias=bias_scaled[:], scale=0.8
                    )
                    nc.sync.dma_start(
                        out[:, k * PIECE + s * width : k * PIECE + (s + 1) * width], squared[:]
                    )
            else:
                positive = work.tile([P, PIECE], F32, name="positive")
                nc.scalar.activation(positive[:], product[:], FUNC.Relu, bias=bias[:])
                h_piece = work.tile([P, PIECE], F32, name="h_piece")
                nc.vector.scalar_tensor_tensor(
                    h_piece[:], product[:], 0.25, positive[:], op0=ALU.mult, op1=ALU.add
                )
                difference = work.tile([P, PIECE], F32, name="difference")
                nc.gpsimd.tensor_tensor(
                    difference[:], h_piece[:], h_centre[:, c * PIECE : (c + 1) * PIECE], ALU.subtract
                )
                squared = work.tile([P, PIECE], F32, name="squared")
                nc.scalar.activation(squared[:], difference[:], FUNC.Square, scale=0.8)
                nc.sync.dma_start(out[:, k * PIECE : (k + 1) * PIECE], squared[:])
